import numpy as np
import ml_dtypes

BF16 = ml_dtypes.bfloat16


def bf(x):
    return np.asarray(x, np.float32).astype(BF16)


def f32(x):
    return np.asarray(x, np.float32)


def f64(x):
    return np.asarray(x).astype(np.float64)


def striped(idx):
    return np.tile(idx.reshape(-1, 16).T, (8, 1))


D, S, H, O, N = 128, 512, 256, 128, 128
BN_EPS = 1e-5
SLOPE = 0.01


def setup_inputs():
    lim1 = np.sqrt(6.0 / (D + H))
    lim2 = np.sqrt(6.0 / (H + O))
    return {
        "table": bf(np.random.standard_normal((D, S))),
        "w1": bf(np.random.uniform(-lim1, lim1, (D, H))),
        "b1": f32(0.1 * np.random.standard_normal((H, 1))),
        "gamma": f32(np.random.uniform(0.5, 1.5, (H, 1))),
        "beta": f32(0.1 * np.random.standard_normal((H, 1))),
        "running_mean": f32(0.1 * np.random.standard_normal((H, 1))),
        "running_var": f32(np.random.uniform(0.5, 1.5, (H, 1))),
        "w2": bf(np.random.uniform(-lim2, lim2, (H, O))),
        "b2": f32(0.1 * np.random.standard_normal((O, 1))),
        "edge_w": f32(np.random.uniform(0.3, 1.0, (1, N))),
        "offs": striped(np.random.permutation(np.tile(np.arange(S), 2))[:N]),
    }


def reference(table, w1, b1, gamma, beta, running_mean, running_var, w2, b2, edge_w, offs):
    idx = offs[:16].T.reshape(-1)
    a = f64(w1).T @ f64(table)[:, idx] + f64(b1)
    l = np.maximum(a, SLOPE * a)
    z = (l - f64(running_mean)) * f64(gamma) / np.sqrt(f64(running_var) + BN_EPS) + f64(beta)
    return f64(edge_w) * (f64(w2).T @ z) + f64(b2)

@@ -1,0 +1,94 @@
+import concourse.mybir as mybir
+
+BF16, F32, U16 = mybir.dt.bfloat16, mybir.dt.float32, mybir.dt.uint16
+ADD, SUBTRACT, MULT, MAX = (
+    mybir.AluOpType.add,
+    mybir.AluOpType.subtract,
+    mybir.AluOpType.mult,
+    mybir.AluOpType.max,
+)
+RSQRT = mybir.ActivationFunctionType.Abs_reciprocal_sqrt
+
+P = 128
+D, S, H, O, N = 128, 512, 256, 128, 128
+HB = H // P
+BN_EPS = 1e-5
+SLOPE = 0.01
+
+FLOPS = 2 * D * H * N + 2 * H * O * N
+
+
+def tile_batchgcn_kernel(
+    tc, table, w1, b1, gamma, beta, running_mean, running_var, w2, b2, edge_w, offs, out
+):
+    nc = tc.nc
+    with (
+        tc.tile_pool(name="held", bufs=1) as held,
+        tc.psum_pool(name="psum", bufs=1) as psum,
+        nc.allow_non_contiguous_dma(reason="per-channel vectors: one float to a partition and block"),
+    ):
+        def per_channel(vector):
+            return vector.rearrange("(p b) one -> p (b one)", b=HB)
+
+        offsets = held.tile([P, N // 16], U16, name="offsets")
+        store = held.tile([D, S], BF16, name="store")
+        w1_loaded = held.tile([D, H], BF16, name="w1_loaded")
+        var = held.tile([P, HB], F32, name="var")
+        bias1 = held.tile([P, HB], F32, name="bias1")
+        mean = held.tile([P, HB], F32, name="mean")
+        gain = held.tile([P, HB], F32, name="gain")
+        offset_bn = held.tile([P, HB], F32, name="offset_bn")
+        proj2 = held.tile([P, HB, O], BF16, name="proj2")
+        edge = held.tile([O, N], F32, name="edge")
+        bias2 = held.tile([O, 1], F32, name="bias2")
+
+        nc.sync.dma_start(offsets[:], offs)
+        nc.sync.dma_start(w1_loaded[:], w1)
+        nc.sync.dma_start(store[:], table)
+        nc.sync.dma_start(var[:], per_channel(running_var))
+        nc.sync.dma_start(bias1[:], per_channel(b1))
+        nc.sync.dma_start(mean[:], per_channel(running_mean))
+        nc.sync.dma_start(gain[:], per_channel(gamma))
+        nc.sync.dma_start(offset_bn[:], per_channel(beta))
+        nc.sync.dma_start(proj2[:], w2.rearrange("(p b) o -> p b o", b=HB))
+        nc.sync.dma_start(edge[:], edge_w.rearrange("one n -> (one n)").partition_broadcast(O))
+        nc.sync.dma_start(bias2[:], b2)
+
+        proj1 = held.tile([D, HB, P], BF16, name="proj1")
+        for b in range(HB):
+            nc.vector.tensor_copy(
+                proj1[:, b, :], w1_loaded[:].rearrange("d (p b) -> d b p", b=HB)[:, b, :]
+            )
+
+        eps = held.tile([P, 1], F32, name="eps")
+        nc.vector.memset(eps[:], BN_EPS)
+        inv_std = held.tile([P, HB], F32, name="inv_std")
+        nc.scalar.activation(inv_std[:], var[:], RSQRT, bias=eps[:])
+        steep = held.tile([P, HB], F32, name="steep")
+        nc.vector.tensor_tensor(steep[:], bias1[:], mean[:], SUBTRACT)
+        flat = held.tile([P, HB], F32, name="flat")
+        nc.vector.scalar_tensor_tensor(flat[:], bias1[:], SLOPE, mean[:], MULT, SUBTRACT)
+        scale = held.tile([P, HB], F32, name="scale")
+        nc.vector.tensor_tensor(scale[:], inv_std[:], gain[:], MULT)
+
+        z = []
+        for b in range(HB):
+            x = psum.tile([P, N], F32, name=f"x{b}")
+            nc.tensor.matmul(x[:], proj1[:, b, :], store[:].indirect(offsets[:]))
+            low = held.tile([P, N], F32, name=f"low{b}")
+            nc.vector.tensor_scalar(low[:], x[:], SLOPE, flat[:, b : b + 1], MULT, ADD)
+            centred = held.tile([P, N], F32, name=f"centred{b}")
+            nc.vector.scalar_tensor_tensor(centred[:], x[:], steep[:, b : b + 1], low[:], ADD, MAX)
+            z_b = held.tile([P, N], BF16, name=f"z{b}")
+            nc.vector.tensor_scalar(
+                z_b[:], centred[:], scale[:, b : b + 1], offset_bn[:, b : b + 1], MULT, ADD
+            )
+            z.append(z_b)
+
+        y = psum.tile([O, N], F32, name="y")
+        for b in range(HB):
+            nc.tensor.matmul(y[:], proj2[:, b, :], z[b][:], start=(b == 0), stop=(b == HB - 1))
+        result = held.tile([O, N], F32, name="result")
+        nc.vector.tensor_tensor(result[:], y[:], edge[:], MULT)
+        nc.vector.tensor_scalar(result[:], result[:], bias2[:], None, ADD)
+        nc.sync.dma_start(out, result[:])

@@ -43,10 +43,10 @@ def tile_batchgcn_kernel(
         bias2 = held.tile([O, 1], F32, name="bias2")
 
         nc.sync.dma_start(offsets[:], offs)
-        nc.sync.dma_start(w1_loaded[:], w1)
-        nc.sync.dma_start(store[:], table)
         nc.sync.dma_start(var[:], per_channel(running_var))
         nc.sync.dma_start(bias1[:], per_channel(b1))
+        nc.sync.dma_start(w1_loaded[:], w1)
+        nc.sync.dma_start(store[:], table)
         nc.sync.dma_start(mean[:], per_channel(running_mean))
         nc.sync.dma_start(gain[:], per_channel(gamma))
         nc.sync.dma_start(offset_bn[:], per_channel(beta))

@@ -32,7 +32,7 @@ def tile_batchgcn_kernel(
 
         offsets = held.tile([P, N // 16], U16, name="offsets")
         store = held.tile([D, S], BF16, name="store")
-        w1_loaded = held.tile([D, H], BF16, name="w1_loaded")
+        proj1 = held.tile([D, H], BF16, name="proj1")
         var = held.tile([P, HB], F32, name="var")
         bias1 = held.tile([P, HB], F32, name="bias1")
         mean = held.tile([P, HB], F32, name="mean")
@@ -45,7 +45,7 @@ def tile_batchgcn_kernel(
         nc.sync.dma_start(offsets[:], offs)
         nc.sync.dma_start(var[:], per_channel(running_var))
         nc.sync.dma_start(bias1[:], per_channel(b1))
-        nc.sync.dma_start(w1_loaded[:], w1)
+        nc.sync.dma_start(proj1[:], w1)
         nc.sync.dma_start(store[:], table)
         nc.sync.dma_start(mean[:], per_channel(running_mean))
         nc.sync.dma_start(gain[:], per_channel(gamma))
@@ -53,12 +53,6 @@ def tile_batchgcn_kernel(
         nc.sync.dma_start(proj2[:], w2.rearrange("(p b) o -> p b o", b=HB))
         nc.sync.dma_start(edge[:], edge_w.rearrange("one n -> (one n)").partition_broadcast(O))
         nc.sync.dma_start(bias2[:], b2)
-
-        proj1 = held.tile([D, HB, P], BF16, name="proj1")
-        for b in range(HB):
-            nc.vector.tensor_copy(
-                proj1[:, b, :], w1_loaded[:].rearrange("d (p b) -> d b p", b=HB)[:, b, :]
-            )
 
         eps = held.tile([P, 1], F32, name="eps")
         nc.vector.memset(eps[:], BN_EPS)
@@ -74,7 +68,7 @@ def tile_batchgcn_kernel(
         z = []
         for b in range(HB):
             x = psum.tile([P, N], F32, name=f"x{b}")
-            nc.tensor.matmul(x[:], proj1[:, b, :], store[:].indirect(offsets[:]))
+            nc.tensor.matmul(x[:], proj1[:, b::HB], store[:].indirect(offsets[:]))
             low = held.tile([P, N], F32, name=f"low{b}")
             nc.vector.tensor_scalar(low[:], x[:], SLOPE, flat[:, b : b + 1], MULT, ADD)
             centred = held.tile([P, N], F32, name=f"centred{b}")

@@ -44,9 +44,9 @@ def tile_batchgcn_kernel(
 
         nc.sync.dma_start(offsets[:], offs)
         nc.sync.dma_start(var[:], per_channel(running_var))
-        nc.sync.dma_start(bias1[:], per_channel(b1))
-        nc.sync.dma_start(proj1[:], w1)
         nc.sync.dma_start(store[:], table)
+        nc.sync.dma_start(proj1[:], w1)
+        nc.sync.dma_start(bias1[:], per_channel(b1))
         nc.sync.dma_start(mean[:], per_channel(running_mean))
         nc.sync.dma_start(gain[:], per_channel(gamma))
         nc.sync.dma_start(offset_bn[:], per_channel(beta))

@@ -79,10 +79,15 @@ def tile_batchgcn_kernel(
             )
             z.append(z_b)
 
-        y = psum.tile([O, N], F32, name="y")
-        for b in range(HB):
-            nc.tensor.matmul(y[:], proj2[:, b, :], z[b][:], start=(b == 0), stop=(b == HB - 1))
         result = held.tile([O, N], F32, name="result")
-        nc.vector.tensor_tensor(result[:], y[:], edge[:], MULT)
-        nc.vector.tensor_scalar(result[:], result[:], bias2[:], None, ADD)
+        half = N // 2
+        for i in range(2):
+            nodes = slice(i * half, (i + 1) * half)
+            y = psum.tile([O, half], F32, name=f"y{i}")
+            for b in range(HB):
+                nc.tensor.matmul(
+                    y[:], proj2[:, b, :], z[b][:, nodes], start=(b == 0), stop=(b == HB - 1)
+                )
+            nc.vector.tensor_tensor(result[:, nodes], y[:], edge[:, nodes], MULT)
+            nc.vector.tensor_scalar(result[:, nodes], result[:, nodes], bias2[:], None, ADD)
         nc.sync.dma_start(out, result[:])

import concourse.mybir as mybir

BF16, F32, U16 = mybir.dt.bfloat16, mybir.dt.float32, mybir.dt.uint16
ADD, SUBTRACT, MULT, MAX = (
    mybir.AluOpType.add,
    mybir.AluOpType.subtract,
    mybir.AluOpType.mult,
    mybir.AluOpType.max,
)
RSQRT = mybir.ActivationFunctionType.Abs_reciprocal_sqrt

P = 128
D, S, H, O, N = 128, 512, 256, 128, 128
HB = H // P
BN_EPS = 1e-5
SLOPE = 0.01

FLOPS = 2 * D * H * N + 2 * H * O * N


def tile_batchgcn_kernel(
    tc, table, w1, b1, gamma, beta, running_mean, running_var, w2, b2, edge_w, offs, out
):
    nc = tc.nc
    with (
        tc.tile_pool(name="held", bufs=1) as held,
        tc.psum_pool(name="psum", bufs=1) as psum,
        nc.allow_non_contiguous_dma(reason="per-channel vectors: one float to a partition and block"),
    ):
        def per_channel(vector):
            return vector.rearrange("(p b) one -> p (b one)", b=HB)

        offsets = held.tile([P, N // 16], U16, name="offsets")
        store = held.tile([D, S], BF16, name="store")
        proj1 = held.tile([D, H], BF16, name="proj1")
        var = held.tile([P, HB], F32, name="var")
        bias1 = held.tile([P, HB], F32, name="bias1")
        mean = held.tile([P, HB], F32, name="mean")
        gain = held.tile([P, HB], F32, name="gain")
        offset_bn = held.tile([P, HB], F32, name="offset_bn")
        proj2 = held.tile([P, HB, O], BF16, name="proj2")
        edge = held.tile([O, N], F32, name="edge")
        bias2 = held.tile([O, 1], F32, name="bias2")

        nc.sync.dma_start(offsets[:], offs)
        nc.sync.dma_start(var[:], per_channel(running_var))
        nc.sync.dma_start(store[:], table)
        nc.sync.dma_start(proj1[:], w1)
        nc.sync.dma_start(bias1[:], per_channel(b1))
        nc.sync.dma_start(mean[:], per_channel(running_mean))
        nc.sync.dma_start(gain[:], per_channel(gamma))
        nc.sync.dma_start(offset_bn[:], per_channel(beta))
        nc.sync.dma_start(proj2[:], w2.rearrange("(p b) o -> p b o", b=HB))
        nc.sync.dma_start(edge[:], edge_w.rearrange("one n -> (one n)").partition_broadcast(O))
        nc.sync.dma_start(bias2[:], b2)

        eps = held.tile([P, 1], F32, name="eps")
        nc.vector.memset(eps[:], BN_EPS)
        inv_std = held.tile([P, HB], F32, name="inv_std")
        nc.scalar.activation(inv_std[:], var[:], RSQRT, bias=eps[:])
        steep = held.tile([P, HB], F32, name="steep")
        nc.vector.tensor_tensor(steep[:], bias1[:], mean[:], SUBTRACT)
        flat = held.tile([P, HB], F32, name="flat")
        nc.vector.scalar_tensor_tensor(flat[:], bias1[:], SLOPE, mean[:], MULT, SUBTRACT)
        scale = held.tile([P, HB], F32, name="scale")
        nc.vector.tensor_tensor(scale[:], inv_std[:], gain[:], MULT)

        z = []
        for b in range(HB):
            x = psum.tile([P, N], F32, name=f"x{b}")
            nc.tensor.matmul(x[:], proj1[:, b::HB], store[:].indirect(offsets[:]))
            low = held.tile([P, N], F32, name=f"low{b}")
            nc.vector.tensor_scalar(low[:], x[:], SLOPE, flat[:, b : b + 1], MULT, ADD)
            centred = held.tile([P, N], F32, name=f"centred{b}")
            nc.vector.scalar_tensor_tensor(centred[:], x[:], steep[:, b : b + 1], low[:], ADD, MAX)
            z_b = held.tile([P, N], BF16, name=f"z{b}")
            nc.vector.tensor_scalar(
                z_b[:], centred[:], scale[:, b : b + 1], offset_bn[:, b : b + 1], MULT, ADD
            )
            z.append(z_b)

        result = held.tile([O, N], F32, name="result")
        half = N // 2
        for i in range(2):
            nodes = slice(i * half, (i + 1) * half)
            y = psum.tile([O, half], F32, name=f"y{i}")
            for b in range(HB):
                nc.tensor.matmul(
                    y[:], proj2[:, b, :], z[b][:, nodes], start=(b == 0), stop=(b == HB - 1)
                )
            nc.vector.tensor_tensor(result[:, nodes], y[:], edge[:, nodes], MULT)
            nc.vector.tensor_scalar(result[:, nodes], result[:, nodes], bias2[:], None, ADD)
        nc.sync.dma_start(out, result[:])
